import numpy as np
import ml_dtypes


def mxq(x, axis, fmt="e4m3"):
    dtype, down = {"e4m3": (ml_dtypes.float8_e4m3fn, 7), "e5m2": (ml_dtypes.float8_e5m2, 14)}[fmt]
    v = np.moveaxis(np.asarray(x, np.float32).astype(ml_dtypes.bfloat16).astype(np.float64), axis, -1)
    blocks = v.reshape(v.shape[:-1] + (-1, 32))
    amax = np.abs(blocks).max(-1, keepdims=True)
    byte = np.maximum(np.where(amax > 0, np.frexp(amax)[1] - 1 + 127, 0) - down, 1)
    scale = np.exp2(byte - 127.0)
    codes = (blocks / scale).astype(np.float32).astype(dtype).astype(np.float64)
    return np.moveaxis((codes * scale).reshape(v.shape), -1, axis)


WIDE = False


def mx_kscale(k):
    if not WIDE:
        return np.ones(k)
    levels = np.array([20, -20, 10, -10, 0])
    a = np.random.permutation(np.resize(levels, k // 512 * 4)).reshape(k // 512, 4)
    idx = np.arange(k)
    return np.exp2(a[idx // 512, idx % 128 // 32])


BF16 = ml_dtypes.bfloat16


def bf(x):
    return np.asarray(x, np.float32).astype(BF16)


def f64(x):
    return np.asarray(x).astype(np.float64)


T, K, N = 2048, 1024, 2048

Q = 127
IN_GRAN = (1, 32)
W_GRAN = (32, 32)


def with_peak(k, gran):
    R, C = k.shape
    gr, gc = gran
    kb = k.reshape(R // gr, gr, C // gc, gc).transpose(0, 2, 1, 3).reshape(-1, gr * gc)
    n = kb.shape[0]
    pos = np.random.randint(0, gr * gc, n)
    sign = 2 * np.random.randint(0, 2, n) - 1
    kb[np.arange(n), pos] = Q * sign
    return kb.reshape(R // gr, C // gc, gr, gc).transpose(0, 2, 1, 3).reshape(R, C)


def setup_inputs():
    g = W_GRAN[0]
    u = np.repeat(mx_kscale(N)[::g], g)
    kx = np.random.randint(-42, 43, (T, K)) + np.random.randint(-42, 43, (T, K)) + np.random.randint(-42, 43, (T, K))
    x = with_peak(kx, IN_GRAN) * 2.0 ** -5
    kw = np.random.randint(-Q, Q + 1, (N, K))
    weight = with_peak(kw, W_GRAN) * 2.0 ** -12 / u[:, None]
    bias = np.random.uniform(-0.5, 0.5, N)
    go = np.random.standard_normal((T, N)) * np.exp2(np.random.randint(-12, 1, (T, 1))) * 16.0 * u[None, :]
    return {"x": bf(x), "weight": bf(weight), "bias": bf(bias), "grad_out": bf(go)}


def reference(x, weight, bias, grad_out):
    return mxq(f64(grad_out), 1, "e5m2") @ mxq(f64(weight), 0, "e4m3")

@@ -1,0 +1,167 @@
+from contextlib import ExitStack
+
+import concourse.mybir as mybir
+from concourse.masks import make_identity
+
+BF16 = mybir.dt.bfloat16
+F32 = mybir.dt.float32
+U32 = mybir.dt.uint32
+U8 = mybir.dt.uint8
+E5M2_X4 = mybir.dt.float8_e5m2_x4
+E4M3_X4 = mybir.dt.float8_e4m3fn_x4
+
+P = 128
+PACK = 4
+K_PASS = P * PACK
+
+TOKENS = 2048
+FEATURES = 2048
+INPUTS = 1024
+
+PASSES = FEATURES // K_PASS
+HALF = 512
+HALVES = INPUTS // HALF
+ROUND_TILES = 2
+ROUND_TOKENS = ROUND_TILES * P
+ROUNDS = TOKENS // ROUND_TOKENS
+WORDS = FEATURES // 2
+TILE_CODES = PASSES * P
+CHUNK = PACK * HALF
+LATE_HALF_AFTER = 4
+
+FLOPS = 2 * TOKENS * FEATURES * INPUTS
+BYTES = 2 * TOKENS * FEATURES + 2 * FEATURES * INPUTS + 4 * TOKENS * INPUTS
+
+
+def tile_linearmem_t_kernel(tc, x, weight, bias, grad_out, out):
+    nc = tc.nc
+    with ExitStack() as ctx:
+        keep = ctx.enter_context(tc.tile_pool(name="keep", bufs=1))
+        raw_pool = ctx.enter_context(tc.tile_pool(name="raw", bufs=ROUNDS))
+        grouped_pool = ctx.enter_context(tc.tile_pool(name="grouped", bufs=4))
+        stage_pool = ctx.enter_context(tc.tile_pool(name="stage", bufs=8))
+        psum = ctx.enter_context(tc.psum_pool(name="psum", bufs=4))
+
+        identity = keep.tile([P, P], F32)
+        make_identity(nc, identity[:])
+
+        g_codes = keep.tile([P, ROUNDS * ROUND_TILES * TILE_CODES], U32, align_bytes=64)
+        g_scales = keep.tile([P, ROUNDS * ROUND_TILES * TILE_CODES], U8, align_bytes=64)
+        w_codes = keep.tile([P, HALVES * PASSES * HALF], U32, align_bytes=64)
+        w_scales = keep.tile([P, HALVES * PASSES * HALF], U8, align_bytes=64)
+        w_raw = keep.tile([P, HALVES * PASSES * CHUNK], BF16)
+
+        def load_grad_out(r):
+            g_raw = raw_pool.tile([P, ROUND_TILES * FEATURES], BF16)
+            rows = grad_out[r * ROUND_TOKENS : (r + 1) * ROUND_TOKENS, :]
+            nc.sync.dma_start(out=g_raw[:], in_=rows.rearrange("(p s) n -> p (s n)", s=ROUND_TILES))
+            return g_raw
+
+        def load_weight_half(h):
+            for g in range(PASSES):
+                for u in range(2):
+                    first = g * K_PASS + u * 2 * P
+                    rows = weight[first : first + 2 * P, h * HALF : (h + 1) * HALF]
+                    start = (h * PASSES + g) * CHUNK + u * 2 * HALF
+                    nc.sync.dma_start(
+                        out=w_raw[:, start : start + 2 * HALF].rearrange("p (e c) -> p e c", e=2),
+                        in_=rows.rearrange("(p e) c -> p e c", e=2),
+                    )
+
+        g_raws = [load_grad_out(0)]
+        load_weight_half(0)
+        for r in range(1, ROUNDS):
+            g_raws.append(load_grad_out(r))
+            if r == LATE_HALF_AFTER:
+                load_weight_half(1)
+
+        def prepare_weight(h, g):
+            chunk = h * PASSES + g
+            rows = w_raw[:, chunk * CHUNK : (chunk + 1) * CHUNK].rearrange("p (t c) -> p t c", t=PACK)
+            w_grouped = grouped_pool.tile([P, CHUNK], BF16, align_bytes=64)
+            cols = w_grouped[:].rearrange("p (c t) -> p c t", t=PACK)
+            middle = HALF // 2
+            nc.vector.tensor_copy(
+                out=cols[:, :middle, :].rearrange("p (c i) t -> p c t i", i=4),
+                in_=rows[:, :, :middle].rearrange("p t (c i) -> p c t i", i=4),
+            )
+            nc.scalar.copy(
+                out=cols[:, middle:, :].rearrange("p (c i) t -> p c t i", i=4),
+                in_=rows[:, :, middle:].rearrange("p t (c i) -> p c t i", i=4),
+            )
+            nc.vector.quantize_mx(
+                out=w_codes[:, chunk * HALF : (chunk + 1) * HALF].bitcast(E4M3_X4),
+                scales=w_scales[:, chunk * HALF : (chunk + 1) * HALF],
+                in_=w_grouped[:],
+            )
+
+        def transpose_round(r):
+            words = g_raws[r][:].bitcast(F32)
+            banks = []
+            for s in range(ROUND_TILES):
+                for pair in range(PASSES // 2):
+                    flipped = psum.tile([P, 4 * P], F32, tag="flipped")
+                    for j in range(4):
+                        first = s * WORDS + (pair * 4 + j) * P
+                        nc.tensor.transpose(
+                            flipped[:, j * P : (j + 1) * P], words[:, first : first + P], identity[:]
+                        )
+                    banks.append(flipped)
+            return banks
+
+        def quantise_round(r, banks):
+            for s in range(ROUND_TILES):
+                g_grouped = grouped_pool.tile([P, PACK * TILE_CODES], BF16, align_bytes=64)
+                pairs = g_grouped[:].bitcast(F32).rearrange("p (g r u) -> p g r u", g=PASSES, u=2)
+                for pair in range(PASSES // 2):
+                    nc.scalar.copy(
+                        out=pairs[:, 2 * pair : 2 * pair + 2, :, :],
+                        in_=banks[s * (PASSES // 2) + pair][:].rearrange("p (g u r) -> p g r u", g=2, u=2),
+                    )
+                m = r * ROUND_TILES + s
+                nc.vector.quantize_mx(
+                    out=g_codes[:, m * TILE_CODES : (m + 1) * TILE_CODES].bitcast(E5M2_X4),
+                    scales=g_scales[:, m * TILE_CODES : (m + 1) * TILE_CODES],
+                    in_=g_grouped[:],
+                )
+
+        def multiply_round(r, h):
+            stage = stage_pool.tile([P, ROUND_TILES * HALF], F32)
+            for s in range(ROUND_TILES):
+                m = r * ROUND_TILES + s
+                acc = psum.tile([P, HALF], F32, tag="acc")
+                for g in range(PASSES):
+                    tokens = slice(m * TILE_CODES + g * P, m * TILE_CODES + (g + 1) * P)
+                    columns = slice((h * PASSES + g) * HALF, (h * PASSES + g + 1) * HALF)
+                    nc.tensor.matmul_mx(
+                        out=acc[:],
+                        lhsT=g_codes[:, tokens].bitcast(E5M2_X4),
+                        lhsT_scale=g_scales[:, tokens],
+                        rhs=w_codes[:, columns].bitcast(E4M3_X4),
+                        rhs_scale=w_scales[:, columns],
+                        start=(g == 0),
+                        stop=(g == PASSES - 1),
+                    )
+                if h == 1 and s == 1:
+                    nc.scalar.copy(out=stage[:, s * HALF : (s + 1) * HALF], in_=acc[:])
+                else:
+                    nc.vector.tensor_copy(out=stage[:, s * HALF : (s + 1) * HALF], in_=acc[:])
+            rows = out[r * ROUND_TOKENS : (r + 1) * ROUND_TOKENS, h * HALF : (h + 1) * HALF]
+            nc.sync.dma_start(
+                out=rows.rearrange("(p s) c -> p s c", s=ROUND_TILES),
+                in_=stage[:].rearrange("p (s c) -> p s c", s=ROUND_TILES),
+            )
+
+        quantise_round(0, transpose_round(0))
+        for g in range(PASSES):
+            prepare_weight(0, g)
+        for r in range(ROUNDS):
+            if r + 1 < ROUNDS:
+                quantise_round(r + 1, transpose_round(r + 1))
+            multiply_round(r, 0)
+            g = r - (ROUNDS - PASSES)
+            if g >= 0:
+                prepare_weight(1, g)
+
+        for r in range(ROUNDS):
+            multiply_round(r, 1)

@@ -21,13 +21,13 @@ INPUTS = 1024
 PASSES = FEATURES // K_PASS
 HALF = 512
 HALVES = INPUTS // HALF
-ROUND_TILES = 2
-ROUND_TOKENS = ROUND_TILES * P
-ROUNDS = TOKENS // ROUND_TOKENS
+TILES = TOKENS // P
 WORDS = FEATURES // 2
 TILE_CODES = PASSES * P
 CHUNK = PACK * HALF
-LATE_HALF_AFTER = 4
+LATE_HALF_AFTER = 9
+LATE_HALF_FROM = 6
+FIRST = 4
 
 FLOPS = 2 * TOKENS * FEATURES * INPUTS
 BYTES = 2 * TOKENS * FEATURES + 2 * FEATURES * INPUTS + 4 * TOKENS * INPUTS
@@ -37,45 +37,47 @@ def tile_linearmem_t_kernel(tc, x, weight, bias, grad_out, out):
     nc = tc.nc
     with ExitStack() as ctx:
         keep = ctx.enter_context(tc.tile_pool(name="keep", bufs=1))
-        raw_pool = ctx.enter_context(tc.tile_pool(name="raw", bufs=ROUNDS))
+        raw_pool = ctx.enter_context(tc.tile_pool(name="raw", bufs=TILES))
         grouped_pool = ctx.enter_context(tc.tile_pool(name="grouped", bufs=4))
-        stage_pool = ctx.enter_context(tc.tile_pool(name="stage", bufs=8))
+        stage_pool = ctx.enter_context(tc.tile_pool(name="stage", bufs=TILES))
         psum = ctx.enter_context(tc.psum_pool(name="psum", bufs=4))
 
         identity = keep.tile([P, P], F32)
         make_identity(nc, identity[:])
 
-        g_codes = keep.tile([P, ROUNDS * ROUND_TILES * TILE_CODES], U32, align_bytes=64)
-        g_scales = keep.tile([P, ROUNDS * ROUND_TILES * TILE_CODES], U8, align_bytes=64)
+        g_codes = keep.tile([P, TILES * TILE_CODES], U32, align_bytes=64)
+        g_scales = keep.tile([P, TILES * TILE_CODES], U8, align_bytes=64)
         w_codes = keep.tile([P, HALVES * PASSES * HALF], U32, align_bytes=64)
         w_scales = keep.tile([P, HALVES * PASSES * HALF], U8, align_bytes=64)
         w_raw = keep.tile([P, HALVES * PASSES * CHUNK], BF16)
 
-        def load_grad_out(r):
-            g_raw = raw_pool.tile([P, ROUND_TILES * FEATURES], BF16)
-            rows = grad_out[r * ROUND_TOKENS : (r + 1) * ROUND_TOKENS, :]
-            nc.sync.dma_start(out=g_raw[:], in_=rows.rearrange("(p s) n -> p (s n)", s=ROUND_TILES))
-            return g_raw
+        spark = keep.tile([P, 8], F32)
+        nc.vector.memset(spark[:], 0.0)
+        warmed = keep.tile([P, 8], F32)
+        nc.scalar.copy(out=warmed[:], in_=spark[:])
 
-        def load_weight_half(h):
-            for g in range(PASSES):
-                for u in range(2):
-                    first = g * K_PASS + u * 2 * P
-                    rows = weight[first : first + 2 * P, h * HALF : (h + 1) * HALF]
-                    start = (h * PASSES + g) * CHUNK + u * 2 * HALF
-                    nc.sync.dma_start(
-                        out=w_raw[:, start : start + 2 * HALF].rearrange("p (e c) -> p e c", e=2),
-                        in_=rows.rearrange("(p e) c -> p e c", e=2),
-                    )
+        g_raws = {}
+        flipped_banks = {}
+        g_groupeds = {}
+        w_groupeds = {}
+        products = {}
 
-        g_raws = [load_grad_out(0)]
-        load_weight_half(0)
-        for r in range(1, ROUNDS):
-            g_raws.append(load_grad_out(r))
-            if r == LATE_HALF_AFTER:
-                load_weight_half(1)
+        def load_grad_out(m):
+            g_raw = raw_pool.tile([P, FEATURES], BF16)
+            nc.sync.dma_start(out=g_raw[:], in_=grad_out[m * P : (m + 1) * P, :])
+            g_raws[m] = g_raw
 
-        def prepare_weight(h, g):
+        def load_weight(h, g):
+            for u in range(2):
+                first = g * K_PASS + u * 2 * P
+                rows = weight[first : first + 2 * P, h * HALF : (h + 1) * HALF]
+                start = (h * PASSES + g) * CHUNK + u * 2 * HALF
+                nc.sync.dma_start(
+                    out=w_raw[:, start : start + 2 * HALF].rearrange("p (e c) -> p e c", e=2),
+                    in_=rows.rearrange("(p e) c -> p e c", e=2),
+                )
+
+        def group_weight(h, g):
             chunk = h * PASSES + g
             rows = w_raw[:, chunk * CHUNK : (chunk + 1) * CHUNK].rearrange("p (t c) -> p t c", t=PACK)
             w_grouped = grouped_pool.tile([P, CHUNK], BF16, align_bytes=64)
@@ -89,79 +91,121 @@ def tile_linearmem_t_kernel(tc, x, weight, bias, grad_out, out):
                 out=cols[:, middle:, :].rearrange("p (c i) t -> p c t i", i=4),
                 in_=rows[:, :, middle:].rearrange("p t (c i) -> p c t i", i=4),
             )
+            w_groupeds[chunk] = w_grouped
+
+        def quantise_weight(h, g):
+            chunk = h * PASSES + g
             nc.vector.quantize_mx(
                 out=w_codes[:, chunk * HALF : (chunk + 1) * HALF].bitcast(E4M3_X4),
                 scales=w_scales[:, chunk * HALF : (chunk + 1) * HALF],
-                in_=w_grouped[:],
+                in_=w_groupeds[chunk][:],
             )
 
-        def transpose_round(r):
-            words = g_raws[r][:].bitcast(F32)
-            banks = []
-            for s in range(ROUND_TILES):
-                for pair in range(PASSES // 2):
-                    flipped = psum.tile([P, 4 * P], F32, tag="flipped")
-                    for j in range(4):
-                        first = s * WORDS + (pair * 4 + j) * P
-                        nc.tensor.transpose(
-                            flipped[:, j * P : (j + 1) * P], words[:, first : first + P], identity[:]
-                        )
-                    banks.append(flipped)
-            return banks
-
-        def quantise_round(r, banks):
-            for s in range(ROUND_TILES):
-                g_grouped = grouped_pool.tile([P, PACK * TILE_CODES], BF16, align_bytes=64)
-                pairs = g_grouped[:].bitcast(F32).rearrange("p (g r u) -> p g r u", g=PASSES, u=2)
-                for pair in range(PASSES // 2):
-                    nc.scalar.copy(
-                        out=pairs[:, 2 * pair : 2 * pair + 2, :, :],
-                        in_=banks[s * (PASSES // 2) + pair][:].rearrange("p (g u r) -> p g r u", g=2, u=2),
-                    )
-                m = r * ROUND_TILES + s
-                nc.vector.quantize_mx(
-                    out=g_codes[:, m * TILE_CODES : (m + 1) * TILE_CODES].bitcast(E5M2_X4),
-                    scales=g_scales[:, m * TILE_CODES : (m + 1) * TILE_CODES],
-                    in_=g_grouped[:],
-                )
-
-        def multiply_round(r, h):
-            stage = stage_pool.tile([P, ROUND_TILES * HALF], F32)
-            for s in range(ROUND_TILES):
-                m = r * ROUND_TILES + s
-                acc = psum.tile([P, HALF], F32, tag="acc")
-                for g in range(PASSES):
-                    tokens = slice(m * TILE_CODES + g * P, m * TILE_CODES + (g + 1) * P)
-                    columns = slice((h * PASSES + g) * HALF, (h * PASSES + g + 1) * HALF)
-                    nc.tensor.matmul_mx(
-                        out=acc[:],
-                        lhsT=g_codes[:, tokens].bitcast(E5M2_X4),
-                        lhsT_scale=g_scales[:, tokens],
-                        rhs=w_codes[:, columns].bitcast(E4M3_X4),
-                        rhs_scale=w_scales[:, columns],
-                        start=(g == 0),
-                        stop=(g == PASSES - 1),
-                    )
-                if h == 1 and s == 1:
-                    nc.scalar.copy(out=stage[:, s * HALF : (s + 1) * HALF], in_=acc[:])
+        def transpose_tile(m, second_bank_on_vector=False):
+            words = g_raws[m][:].bitcast(F32)
+            g_grouped = grouped_pool.tile([P, PACK * TILE_CODES], BF16, align_bytes=64)
+            pairs = g_grouped[:].bitcast(F32).rearrange("p (g r u) -> p g r u", g=PASSES, u=2)
+            for pair in range(PASSES // 2):
+                flipped = psum.tile([P, 4 * P], F32, tag="flipped")
+                for j in range(4):
+                    first = (pair * 4 + j) * P
+                    nc.tensor.transpose(flipped[:, j * P : (j + 1) * P], words[:, first : first + P], identity[:])
+                dst = pairs[:, 2 * pair : 2 * pair + 2, :, :]
+                src = flipped[:].rearrange("p (g u r) -> p g r u", g=2, u=2)
+                if pair == 1 and second_bank_on_vector:
+                    nc.vector.tensor_copy(out=dst, in_=src)
                 else:
-                    nc.vector.tensor_copy(out=stage[:, s * HALF : (s + 1) * HALF], in_=acc[:])
-            rows = out[r * ROUND_TOKENS : (r + 1) * ROUND_TOKENS, h * HALF : (h + 1) * HALF]
-            nc.sync.dma_start(
-                out=rows.rearrange("(p s) c -> p s c", s=ROUND_TILES),
-                in_=stage[:].rearrange("p (s c) -> p s c", s=ROUND_TILES),
+                    nc.scalar.copy(out=dst, in_=src)
+            g_groupeds[m] = g_grouped
+
+        def quantise_tile(m):
+            nc.vector.quantize_mx(
+                out=g_codes[:, m * TILE_CODES : (m + 1) * TILE_CODES].bitcast(E5M2_X4),
+                scales=g_scales[:, m * TILE_CODES : (m + 1) * TILE_CODES],
+                in_=g_groupeds[m][:],
             )
 
-        quantise_round(0, transpose_round(0))
-        for g in range(PASSES):
-            prepare_weight(0, g)
-        for r in range(ROUNDS):
-            if r + 1 < ROUNDS:
-                quantise_round(r + 1, transpose_round(r + 1))
-            multiply_round(r, 0)
-            g = r - (ROUNDS - PASSES)
-            if g >= 0:
-                prepare_weight(1, g)
+        def multiply(m, h, g):
+            if g == 0:
+                acc = psum.tile([P, HALF], F32, tag="acc")
+                products[m, h] = acc
+            tokens = slice(m * TILE_CODES + g * P, m * TILE_CODES + (g + 1) * P)
+            columns = slice((h * PASSES + g) * HALF, (h * PASSES + g + 1) * HALF)
+            nc.tensor.matmul_mx(
+                out=products[m, h][:],
+                lhsT=g_codes[:, tokens].bitcast(E5M2_X4),
+                lhsT_scale=g_scales[:, tokens],
+                rhs=w_codes[:, columns].bitcast(E4M3_X4),
+                rhs_scale=w_scales[:, columns],
+                start=(g == 0),
+                stop=(g == PASSES - 1),
+            )
 
-        for r in range(ROUNDS):
-            multiply_round(r, 1)
+        def store(m, h, on_scalar):
+            stage = stage_pool.tile([P, HALF], F32)
+            if on_scalar:
+                nc.scalar.copy(out=stage[:], in_=products[m, h][:])
+            else:
+                nc.vector.tensor_copy(out=stage[:], in_=products[m, h][:])
+            nc.sync.dma_start(out=out[m * P : (m + 1) * P, h * HALF : (h + 1) * HALF], in_=stage[:])
+
+        ctx.enter_context(tc.manual_schedule())
+
+        for m in range(FIRST - 1):
+            load_grad_out(m)
+        load_weight(0, 0)
+        load_grad_out(FIRST - 1)
+        for g in range(1, PASSES):
+            load_weight(0, g)
+        for m in range(FIRST, TILES):
+            load_grad_out(m)
+            if m == LATE_HALF_AFTER:
+                for g in range(PASSES):
+                    load_weight(1, g)
+
+        for m in range(FIRST - 1):
+            transpose_tile(m, second_bank_on_vector=(m < 2))
+        quantise_tile(0)
+        group_weight(0, 0)
+        transpose_tile(FIRST - 1)
+        quantise_tile(1)
+        quantise_tile(2)
+        for g in range(PASSES):
+            if g + 1 < PASSES:
+                group_weight(0, g + 1)
+            quantise_weight(0, g)
+            if g == 0:
+                quantise_tile(3)
+        for g in range(PASSES):
+            if g == PASSES // 2:
+                transpose_tile(FIRST)
+                transpose_tile(FIRST + 1)
+            for m in range(FIRST):
+                multiply(m, 0, g)
+        quantise_tile(FIRST)
+        quantise_tile(FIRST + 1)
+        for m in range(FIRST):
+            store(m, 0, on_scalar=(m % 2 == 0))
+
+        for m in range(FIRST, TILES, 2):
+            more = m + 2 < TILES
+            if more:
+                transpose_tile(m + 2)
+                transpose_tile(m + 3)
+            for s in (m, m + 1):
+                for g in range(PASSES):
+                    multiply(s, 0, g)
+            if more:
+                quantise_tile(m + 2)
+                quantise_tile(m + 3)
+            store(m, 0, on_scalar=False)
+            store(m + 1, 0, on_scalar=False)
+            g = (m - LATE_HALF_FROM) // 2
+            if 0 <= g < PASSES:
+                group_weight(1, g)
+                quantise_weight(1, g)
+
+        for m in range(TILES):
+            for g in range(PASSES):
+                multiply(m, 1, g)
+            store(m, 1, on_scalar=(m % 2 == 0))

@@ -51,10 +51,10 @@ def tile_linearmem_t_kernel(tc, x, weight, bias, grad_out, out):
         w_scales = keep.tile([P, HALVES * PASSES * HALF], U8, align_bytes=64)
         w_raw = keep.tile([P, HALVES * PASSES * CHUNK], BF16)
 
-        spark = keep.tile([P, 8], F32)
-        nc.vector.memset(spark[:], 0.0)
-        warmed = keep.tile([P, 8], F32)
-        nc.scalar.copy(out=warmed[:], in_=spark[:])
+        zeros = keep.tile([P, HALF], BF16)
+        nc.vector.memset(zeros[:], 0.0)
+        table_loaded = keep.tile([P, 8], BF16)
+        nc.scalar.copy(out=table_loaded[:], in_=zeros[:, :8])
 
         g_raws = {}
         flipped_banks = {}
@@ -149,6 +149,11 @@ def tile_linearmem_t_kernel(tc, x, weight, bias, grad_out, out):
                 nc.vector.tensor_copy(out=stage[:], in_=products[m, h][:])
             nc.sync.dma_start(out=out[m * P : (m + 1) * P, h * HALF : (h + 1) * HALF], in_=stage[:])
 
+        def warm_up(count):
+            idle = psum.tile([P, HALF], F32, tag="acc")
+            for i in range(count):
+                nc.tensor.matmul(idle[:], lhsT=zeros[:, :P], rhs=zeros[:], start=True, stop=True)
+
         ctx.enter_context(tc.manual_schedule())
 
         for m in range(FIRST - 1):
@@ -163,11 +168,13 @@ def tile_linearmem_t_kernel(tc, x, weight, bias, grad_out, out):
                 for g in range(PASSES):
                     load_weight(1, g)
 
+        warm_up(4)
         for m in range(FIRST - 1):
             transpose_tile(m, second_bank_on_vector=(m < 2))
         quantise_tile(0)
         group_weight(0, 0)
         transpose_tile(FIRST - 1)
+        warm_up(4)
         quantise_tile(1)
         quantise_tile(2)
         for g in range(PASSES):

@@ -25,8 +25,7 @@ TILES = TOKENS // P
 WORDS = FEATURES // 2
 TILE_CODES = PASSES * P
 CHUNK = PACK * HALF
-LATE_HALF_AFTER = 9
-LATE_HALF_FROM = 6
+LATE_HALF_AFTER = 7
 FIRST = 4
 
 FLOPS = 2 * TOKENS * FEATURES * INPUTS
@@ -77,28 +76,29 @@ def tile_linearmem_t_kernel(tc, x, weight, bias, grad_out, out):
                     in_=rows.rearrange("(p e) c -> p e c", e=2),
                 )
 
-        def group_weight(h, g):
+        def group_weight(h, g, first=0, count=HALF):
             chunk = h * PASSES + g
             rows = w_raw[:, chunk * CHUNK : (chunk + 1) * CHUNK].rearrange("p (t c) -> p t c", t=PACK)
-            w_grouped = grouped_pool.tile([P, CHUNK], BF16, align_bytes=64)
+            w_grouped = grouped_pool.tile([P, PACK * count], BF16, align_bytes=64)
             cols = w_grouped[:].rearrange("p (c t) -> p c t", t=PACK)
-            middle = HALF // 2
+            middle = count // 2
             nc.vector.tensor_copy(
                 out=cols[:, :middle, :].rearrange("p (c i) t -> p c t i", i=4),
-                in_=rows[:, :, :middle].rearrange("p t (c i) -> p c t i", i=4),
+                in_=rows[:, :, first : first + middle].rearrange("p t (c i) -> p c t i", i=4),
             )
             nc.scalar.copy(
                 out=cols[:, middle:, :].rearrange("p (c i) t -> p c t i", i=4),
-                in_=rows[:, :, middle:].rearrange("p t (c i) -> p c t i", i=4),
+                in_=rows[:, :, first + middle : first + count].rearrange("p t (c i) -> p c t i", i=4),
             )
-            w_groupeds[chunk] = w_grouped
+            w_groupeds[chunk, first] = w_grouped
 
-        def quantise_weight(h, g):
+        def quantise_weight(h, g, first=0, count=HALF):
             chunk = h * PASSES + g
+            columns = slice(chunk * HALF + first, chunk * HALF + first + count)
             nc.vector.quantize_mx(
-                out=w_codes[:, chunk * HALF : (chunk + 1) * HALF].bitcast(E4M3_X4),
-                scales=w_scales[:, chunk * HALF : (chunk + 1) * HALF],
-                in_=w_groupeds[chunk][:],
+                out=w_codes[:, columns].bitcast(E4M3_X4),
+                scales=w_scales[:, columns],
+                in_=w_groupeds[chunk, first][:],
             )
 
         def transpose_tile(m, second_bank_on_vector=False):
@@ -164,9 +164,8 @@ def tile_linearmem_t_kernel(tc, x, weight, bias, grad_out, out):
             load_weight(0, g)
         for m in range(FIRST, TILES):
             load_grad_out(m)
-            if m == LATE_HALF_AFTER:
-                for g in range(PASSES):
-                    load_weight(1, g)
+            if m >= LATE_HALF_AFTER and (m - LATE_HALF_AFTER) % 2 == 0 and m + 1 < TILES:
+                load_weight(1, (m - LATE_HALF_AFTER) // 2)
 
         warm_up(4)
         for m in range(FIRST - 1):
@@ -207,12 +206,18 @@ def tile_linearmem_t_kernel(tc, x, weight, bias, grad_out, out):
                 quantise_tile(m + 3)
             store(m, 0, on_scalar=False)
             store(m + 1, 0, on_scalar=False)
-            g = (m - LATE_HALF_FROM) // 2
-            if 0 <= g < PASSES:
-                group_weight(1, g)
-                quantise_weight(1, g)
+            step = (m - FIRST) // 2
+            for piece in range(step, step + 1 if more else 2 * PASSES):
+                g, first = piece // 2, piece % 2 * (HALF // 2)
+                group_weight(1, g, first, HALF // 2)
+                quantise_weight(1, g, first, HALF // 2)
 
-        for m in range(TILES):
+        for g in range(PASSES):
+            for m in range(FIRST):
+                multiply(m, 1, g)
+        for m in range(FIRST):
+            store(m, 1, on_scalar=(m % 2 == 0))
+        for m in range(FIRST, TILES):
             for g in range(PASSES):
                 multiply(m, 1, g)
             store(m, 1, on_scalar=(m % 2 == 0))

@@ -127,7 +127,8 @@ def tile_linearmem_t_kernel(tc, x, weight, bias, grad_out, out):
 
         def multiply(m, h, g):
             if g == 0:
-                acc = psum.tile([P, HALF], F32, tag="acc")
+                tag = "flipped" if h == 1 and m // FIRST % 2 == 1 else "acc"
+                acc = psum.tile([P, HALF], F32, tag=tag)
                 products[m, h] = acc
             tokens = slice(m * TILE_CODES + g * P, m * TILE_CODES + (g + 1) * P)
             columns = slice((h * PASSES + g) * HALF, (h * PASSES + g + 1) * HALF)

@@ -127,7 +127,7 @@ def tile_linearmem_t_kernel(tc, x, weight, bias, grad_out, out):
 
         def multiply(m, h, g):
             if g == 0:
-                tag = "flipped" if h == 1 and m // FIRST % 2 == 1 else "acc"
+                tag = "flipped" if h == 1 and m // FIRST % 2 == 0 else "acc"
                 acc = psum.tile([P, HALF], F32, tag=tag)
                 products[m, h] = acc
             tokens = slice(m * TILE_CODES + g * P, m * TILE_CODES + (g + 1) * P)
@@ -171,10 +171,11 @@ def tile_linearmem_t_kernel(tc, x, weight, bias, grad_out, out):
         warm_up(4)
         for m in range(FIRST - 1):
             transpose_tile(m, second_bank_on_vector=(m < 2))
+            warm_up(2)
         quantise_tile(0)
         group_weight(0, 0)
         transpose_tile(FIRST - 1)
-        warm_up(4)
+        warm_up(2)
         quantise_tile(1)
         quantise_tile(2)
         for g in range(PASSES):
@@ -205,13 +206,13 @@ def tile_linearmem_t_kernel(tc, x, weight, bias, grad_out, out):
             if more:
                 quantise_tile(m + 2)
                 quantise_tile(m + 3)
-            store(m, 0, on_scalar=False)
-            store(m + 1, 0, on_scalar=False)
             step = (m - FIRST) // 2
-            for piece in range(step, step + 1 if more else 2 * PASSES):
+            for piece in range(step + max(0, step - 4), step + 1 + max(0, step - 3)):
                 g, first = piece // 2, piece % 2 * (HALF // 2)
                 group_weight(1, g, first, HALF // 2)
                 quantise_weight(1, g, first, HALF // 2)
+            store(m, 0, on_scalar=False)
+            store(m + 1, 0, on_scalar=False)
 
         for g in range(PASSES):
             for m in range(FIRST):

@@ -197,15 +197,13 @@ def tile_linearmem_t_kernel(tc, x, weight, bias, grad_out, out):
 
         for m in range(FIRST, TILES, 2):
             more = m + 2 < TILES
-            if more:
-                transpose_tile(m + 2)
-                transpose_tile(m + 3)
             for s in (m, m + 1):
+                if more:
+                    transpose_tile(s + 2)
                 for g in range(PASSES):
                     multiply(s, 0, g)
-            if more:
-                quantise_tile(m + 2)
-                quantise_tile(m + 3)
+                if more:
+                    quantise_tile(s + 2)
             step = (m - FIRST) // 2
             for piece in range(step + max(0, step - 4), step + 1 + max(0, step - 3)):
                 g, first = piece // 2, piece % 2 * (HALF // 2)

from contextlib import ExitStack

import concourse.mybir as mybir
from concourse.masks import make_identity

BF16 = mybir.dt.bfloat16
F32 = mybir.dt.float32
U32 = mybir.dt.uint32
U8 = mybir.dt.uint8
E5M2_X4 = mybir.dt.float8_e5m2_x4
E4M3_X4 = mybir.dt.float8_e4m3fn_x4

P = 128
PACK = 4
K_PASS = P * PACK

TOKENS = 2048
FEATURES = 2048
INPUTS = 1024

PASSES = FEATURES // K_PASS
HALF = 512
HALVES = INPUTS // HALF
TILES = TOKENS // P
WORDS = FEATURES // 2
TILE_CODES = PASSES * P
CHUNK = PACK * HALF
LATE_HALF_AFTER = 7
FIRST = 4

FLOPS = 2 * TOKENS * FEATURES * INPUTS
BYTES = 2 * TOKENS * FEATURES + 2 * FEATURES * INPUTS + 4 * TOKENS * INPUTS


def tile_linearmem_t_kernel(tc, x, weight, bias, grad_out, out):
    nc = tc.nc
    with ExitStack() as ctx:
        keep = ctx.enter_context(tc.tile_pool(name="keep", bufs=1))
        raw_pool = ctx.enter_context(tc.tile_pool(name="raw", bufs=TILES))
        grouped_pool = ctx.enter_context(tc.tile_pool(name="grouped", bufs=4))
        stage_pool = ctx.enter_context(tc.tile_pool(name="stage", bufs=TILES))
        psum = ctx.enter_context(tc.psum_pool(name="psum", bufs=4))

        identity = keep.tile([P, P], F32)
        make_identity(nc, identity[:])

        g_codes = keep.tile([P, TILES * TILE_CODES], U32, align_bytes=64)
        g_scales = keep.tile([P, TILES * TILE_CODES], U8, align_bytes=64)
        w_codes = keep.tile([P, HALVES * PASSES * HALF], U32, align_bytes=64)
        w_scales = keep.tile([P, HALVES * PASSES * HALF], U8, align_bytes=64)
        w_raw = keep.tile([P, HALVES * PASSES * CHUNK], BF16)

        zeros = keep.tile([P, HALF], BF16)
        nc.vector.memset(zeros[:], 0.0)
        table_loaded = keep.tile([P, 8], BF16)
        nc.scalar.copy(out=table_loaded[:], in_=zeros[:, :8])

        g_raws = {}
        flipped_banks = {}
        g_groupeds = {}
        w_groupeds = {}
        products = {}

        def load_grad_out(m):
            g_raw = raw_pool.tile([P, FEATURES], BF16)
            nc.sync.dma_start(out=g_raw[:], in_=grad_out[m * P : (m + 1) * P, :])
            g_raws[m] = g_raw

        def load_weight(h, g):
            for u in range(2):
                first = g * K_PASS + u * 2 * P
                rows = weight[first : first + 2 * P, h * HALF : (h + 1) * HALF]
                start = (h * PASSES + g) * CHUNK + u * 2 * HALF
                nc.sync.dma_start(
                    out=w_raw[:, start : start + 2 * HALF].rearrange("p (e c) -> p e c", e=2),
                    in_=rows.rearrange("(p e) c -> p e c", e=2),
                )

        def group_weight(h, g, first=0, count=HALF):
            chunk = h * PASSES + g
            rows = w_raw[:, chunk * CHUNK : (chunk + 1) * CHUNK].rearrange("p (t c) -> p t c", t=PACK)
            w_grouped = grouped_pool.tile([P, PACK * count], BF16, align_bytes=64)
            cols = w_grouped[:].rearrange("p (c t) -> p c t", t=PACK)
            middle = count // 2
            nc.vector.tensor_copy(
                out=cols[:, :middle, :].rearrange("p (c i) t -> p c t i", i=4),
                in_=rows[:, :, first : first + middle].rearrange("p t (c i) -> p c t i", i=4),
            )
            nc.scalar.copy(
                out=cols[:, middle:, :].rearrange("p (c i) t -> p c t i", i=4),
                in_=rows[:, :, first + middle : first + count].rearrange("p t (c i) -> p c t i", i=4),
            )
            w_groupeds[chunk, first] = w_grouped

        def quantise_weight(h, g, first=0, count=HALF):
            chunk = h * PASSES + g
            columns = slice(chunk * HALF + first, chunk * HALF + first + count)
            nc.vector.quantize_mx(
                out=w_codes[:, columns].bitcast(E4M3_X4),
                scales=w_scales[:, columns],
                in_=w_groupeds[chunk, first][:],
            )

        def transpose_tile(m, second_bank_on_vector=False):
            words = g_raws[m][:].bitcast(F32)
            g_grouped = grouped_pool.tile([P, PACK * TILE_CODES], BF16, align_bytes=64)
            pairs = g_grouped[:].bitcast(F32).rearrange("p (g r u) -> p g r u", g=PASSES, u=2)
            for pair in range(PASSES // 2):
                flipped = psum.tile([P, 4 * P], F32, tag="flipped")
                for j in range(4):
                    first = (pair * 4 + j) * P
                    nc.tensor.transpose(flipped[:, j * P : (j + 1) * P], words[:, first : first + P], identity[:])
                dst = pairs[:, 2 * pair : 2 * pair + 2, :, :]
                src = flipped[:].rearrange("p (g u r) -> p g r u", g=2, u=2)
                if pair == 1 and second_bank_on_vector:
                    nc.vector.tensor_copy(out=dst, in_=src)
                else:
                    nc.scalar.copy(out=dst, in_=src)
            g_groupeds[m] = g_grouped

        def quantise_tile(m):
            nc.vector.quantize_mx(
                out=g_codes[:, m * TILE_CODES : (m + 1) * TILE_CODES].bitcast(E5M2_X4),
                scales=g_scales[:, m * TILE_CODES : (m + 1) * TILE_CODES],
                in_=g_groupeds[m][:],
            )

        def multiply(m, h, g):
            if g == 0:
                tag = "flipped" if h == 1 and m // FIRST % 2 == 0 else "acc"
                acc = psum.tile([P, HALF], F32, tag=tag)
                products[m, h] = acc
            tokens = slice(m * TILE_CODES + g * P, m * TILE_CODES + (g + 1) * P)
            columns = slice((h * PASSES + g) * HALF, (h * PASSES + g + 1) * HALF)
            nc.tensor.matmul_mx(
                out=products[m, h][:],
                lhsT=g_codes[:, tokens].bitcast(E5M2_X4),
                lhsT_scale=g_scales[:, tokens],
                rhs=w_codes[:, columns].bitcast(E4M3_X4),
                rhs_scale=w_scales[:, columns],
                start=(g == 0),
                stop=(g == PASSES - 1),
            )

        def store(m, h, on_scalar):
            stage = stage_pool.tile([P, HALF], F32)
            if on_scalar:
                nc.scalar.copy(out=stage[:], in_=products[m, h][:])
            else:
                nc.vector.tensor_copy(out=stage[:], in_=products[m, h][:])
            nc.sync.dma_start(out=out[m * P : (m + 1) * P, h * HALF : (h + 1) * HALF], in_=stage[:])

        def warm_up(count):
            idle = psum.tile([P, HALF], F32, tag="acc")
            for i in range(count):
                nc.tensor.matmul(idle[:], lhsT=zeros[:, :P], rhs=zeros[:], start=True, stop=True)

        ctx.enter_context(tc.manual_schedule())

        for m in range(FIRST - 1):
            load_grad_out(m)
        load_weight(0, 0)
        load_grad_out(FIRST - 1)
        for g in range(1, PASSES):
            load_weight(0, g)
        for m in range(FIRST, TILES):
            load_grad_out(m)
            if m >= LATE_HALF_AFTER and (m - LATE_HALF_AFTER) % 2 == 0 and m + 1 < TILES:
                load_weight(1, (m - LATE_HALF_AFTER) // 2)

        warm_up(4)
        for m in range(FIRST - 1):
            transpose_tile(m, second_bank_on_vector=(m < 2))
            warm_up(2)
        quantise_tile(0)
        group_weight(0, 0)
        transpose_tile(FIRST - 1)
        warm_up(2)
        quantise_tile(1)
        quantise_tile(2)
        for g in range(PASSES):
            if g + 1 < PASSES:
                group_weight(0, g + 1)
            quantise_weight(0, g)
            if g == 0:
                quantise_tile(3)
        for g in range(PASSES):
            if g == PASSES // 2:
                transpose_tile(FIRST)
                transpose_tile(FIRST + 1)
            for m in range(FIRST):
                multiply(m, 0, g)
        quantise_tile(FIRST)
        quantise_tile(FIRST + 1)
        for m in range(FIRST):
            store(m, 0, on_scalar=(m % 2 == 0))

        for m in range(FIRST, TILES, 2):
            more = m + 2 < TILES
            for s in (m, m + 1):
                if more:
                    transpose_tile(s + 2)
                for g in range(PASSES):
                    multiply(s, 0, g)
                if more:
                    quantise_tile(s + 2)
            step = (m - FIRST) // 2
            for piece in range(step + max(0, step - 4), step + 1 + max(0, step - 3)):
                g, first = piece // 2, piece % 2 * (HALF // 2)
                group_weight(1, g, first, HALF // 2)
                quantise_weight(1, g, first, HALF // 2)
            store(m, 0, on_scalar=False)
            store(m + 1, 0, on_scalar=False)

        for g in range(PASSES):
            for m in range(FIRST):
                multiply(m, 1, g)
        for m in range(FIRST):
            store(m, 1, on_scalar=(m % 2 == 0))
        for m in range(FIRST, TILES):
            for g in range(PASSES):
                multiply(m, 1, g)
            store(m, 1, on_scalar=(m % 2 == 0))
